import numpy as np
import ml_dtypes

BF16 = ml_dtypes.bfloat16


def bf(x):
    return np.asarray(x, np.float32).astype(BF16)


def f32(x):
    return np.asarray(x, np.float32)


def f64(x):
    return np.asarray(x).astype(np.float64)


def striped(idx):
    return np.tile(idx.reshape(-1, 16).T, (8, 1))


C, S, B, L, N = 256, 4096, 2, 1024, 2048


def setup_inputs():
    return {"tok": f32(np.random.standard_normal((C, S))), "pos": f32(np.random.standard_normal((C, L))), "phase": f32(0.1 * np.random.standard_normal((C, 1))), "offs": striped(np.random.permutation(np.tile(np.arange(S), 2))[:N])}


def reference(tok, pos, phase, offs):
    idx = offs[:16].T.reshape(-1)
    phi = np.pi * np.tanh(f64(phase))
    rot = np.cos(phi) - np.sin(phi)
    return (f64(tok)[:, idx] + np.tile(f64(pos), (1, B))) * rot

@@ -1,0 +1,61 @@
+import math
+
+import concourse.mybir as mybir
+
+F32 = mybir.dt.float32
+U16 = mybir.dt.uint16
+ADD = mybir.AluOpType.add
+ACT = mybir.ActivationFunctionType
+
+P = 128
+PER_COLUMN = 16
+
+
+def tile_quantuminspiredllm_kernel(tc, tok, pos, phase, offs, out):
+    nc = tc.nc
+    channels, words = tok.shape
+    length = pos.shape[1]
+    entries = out.shape[1]
+    blocks = channels // P
+    sequences = entries // length
+
+    with (
+        tc.tile_pool(name="held", bufs=1) as held,
+        tc.tile_pool(name="work", bufs=4) as work,
+    ):
+        offsets = held.tile([P, entries // PER_COLUMN], U16, name="offsets")
+        nc.sync.dma_start(offsets[:], offs)
+
+        phases = held.tile([P, blocks], F32, name="phases")
+        with nc.allow_non_contiguous_dma(reason="one float32 to a partition, 256 in all"):
+            nc.scalar.dma_start(phases[:], phase.rearrange("(b p) o -> p (b o)", p=P))
+
+        tables = []
+        positions = []
+        for b in range(blocks):
+            rows = slice(b * P, (b + 1) * P)
+            table = held.tile([P, words], F32, name=f"table{b}")
+            nc.sync.dma_start(table[:], tok[rows, :])
+            tables.append(table)
+            position = held.tile([P, length], F32, name=f"position{b}")
+            nc.sync.dma_start(position[:], pos[rows, :])
+            positions.append(position)
+
+        rot = held.tile([P, blocks], F32, name="rot")
+        nc.scalar.activation(rot[:], phases[:], ACT.Tanh)
+        nc.scalar.activation(rot[:], rot[:], ACT.Abs, bias=0.25)
+        nc.scalar.activation(rot[:], rot[:], ACT.Sin, bias=math.pi / 2, scale=-math.pi)
+        nc.scalar.mul(rot[:], rot[:], math.sqrt(2.0))
+
+        for b in range(blocks):
+            rows = slice(b * P, (b + 1) * P)
+            for s in range(sequences):
+                piece = slice(s * length, (s + 1) * length)
+                piece_offsets = offsets[:, s * length // PER_COLUMN : (s + 1) * length // PER_COLUMN]
+                summed = work.tile([P, length], F32, name="summed")
+                nc.vector.tensor_tensor(
+                    summed[:], tables[b][:].indirect(piece_offsets), positions[b][:], ADD
+                )
+                rotated = work.tile([P, length], F32, name="rotated")
+                nc.scalar.activation(rotated[:], summed[:], ACT.Identity, scale=rot[:, b : b + 1])
+                nc.sync.dma_start(out[rows, piece], rotated[:])

@@ -9,6 +9,7 @@ ACT = mybir.ActivationFunctionType
 
 P = 128
 PER_COLUMN = 16
+PIECE = 512
 
 
 def tile_quantuminspiredllm_kernel(tc, tok, pos, phase, offs, out):
@@ -17,7 +18,6 @@ def tile_quantuminspiredllm_kernel(tc, tok, pos, phase, offs, out):
     length = pos.shape[1]
     entries = out.shape[1]
     blocks = channels // P
-    sequences = entries // length
 
     with (
         tc.tile_pool(name="held", bufs=1) as held,
@@ -49,13 +49,16 @@ def tile_quantuminspiredllm_kernel(tc, tok, pos, phase, offs, out):
 
         for b in range(blocks):
             rows = slice(b * P, (b + 1) * P)
-            for s in range(sequences):
-                piece = slice(s * length, (s + 1) * length)
-                piece_offsets = offsets[:, s * length // PER_COLUMN : (s + 1) * length // PER_COLUMN]
-                summed = work.tile([P, length], F32, name="summed")
+            for first in range(0, entries, PIECE):
+                piece_offsets = offsets[:, first // PER_COLUMN : (first + PIECE) // PER_COLUMN]
+                where = first % length
+                summed = work.tile([P, PIECE], F32, name="summed")
                 nc.vector.tensor_tensor(
-                    summed[:], tables[b][:].indirect(piece_offsets), positions[b][:], ADD
+                    summed[:],
+                    tables[b][:].indirect(piece_offsets),
+                    positions[b][:, where : where + PIECE],
+                    ADD,
                 )
-                rotated = work.tile([P, length], F32, name="rotated")
+                rotated = work.tile([P, PIECE], F32, name="rotated")
                 nc.scalar.activation(rotated[:], summed[:], ACT.Identity, scale=rot[:, b : b + 1])
-                nc.sync.dma_start(out[rows, piece], rotated[:])
+                nc.sync.dma_start(out[rows, first : first + PIECE], rotated[:])

@@ -18,10 +18,12 @@ def tile_quantuminspiredllm_kernel(tc, tok, pos, phase, offs, out):
     length = pos.shape[1]
     entries = out.shape[1]
     blocks = channels // P
+    sequences = entries // length
+    spans = length // PIECE
 
     with (
         tc.tile_pool(name="held", bufs=1) as held,
-        tc.tile_pool(name="work", bufs=4) as work,
+        tc.tile_pool(name="work", bufs=blocks * sequences * spans) as work,
     ):
         offsets = held.tile([P, entries // PER_COLUMN], U16, name="offsets")
         nc.sync.dma_start(offsets[:], offs)
@@ -37,9 +39,10 @@ def tile_quantuminspiredllm_kernel(tc, tok, pos, phase, offs, out):
             table = held.tile([P, words], F32, name=f"table{b}")
             nc.sync.dma_start(table[:], tok[rows, :])
             tables.append(table)
-            position = held.tile([P, length], F32, name=f"position{b}")
-            nc.sync.dma_start(position[:], pos[rows, :])
-            positions.append(position)
+            for h in range(spans):
+                position = held.tile([P, PIECE], F32, name=f"position{b}_{h}")
+                nc.sync.dma_start(position[:], pos[rows, h * PIECE : (h + 1) * PIECE])
+                positions.append(position)
 
         rot = held.tile([P, blocks], F32, name="rot")
         nc.scalar.activation(rot[:], phases[:], ACT.Tanh)
@@ -49,16 +52,16 @@ def tile_quantuminspiredllm_kernel(tc, tok, pos, phase, offs, out):
 
         for b in range(blocks):
             rows = slice(b * P, (b + 1) * P)
-            for first in range(0, entries, PIECE):
-                piece_offsets = offsets[:, first // PER_COLUMN : (first + PIECE) // PER_COLUMN]
-                where = first % length
-                summed = work.tile([P, PIECE], F32, name="summed")
-                nc.vector.tensor_tensor(
-                    summed[:],
-                    tables[b][:].indirect(piece_offsets),
-                    positions[b][:, where : where + PIECE],
-                    ADD,
-                )
-                rotated = work.tile([P, PIECE], F32, name="rotated")
-                nc.scalar.activation(rotated[:], summed[:], ACT.Identity, scale=rot[:, b : b + 1])
-                nc.sync.dma_start(out[rows, first : first + PIECE], rotated[:])
+            for h in range(spans):
+                for s in range(sequences):
+                    first = s * length + h * PIECE
+                    piece_offsets = offsets[:, first // PER_COLUMN : (first + PIECE) // PER_COLUMN]
+                    piece = work.tile([P, PIECE], F32, name="piece")
+                    nc.vector.tensor_tensor(
+                        piece[:],
+                        tables[b][:].indirect(piece_offsets),
+                        positions[b * spans + h][:],
+                        ADD,
+                    )
+                    nc.scalar.activation(piece[:], piece[:], ACT.Identity, scale=rot[:, b : b + 1])
+                    nc.sync.dma_start(out[rows, first : first + PIECE], piece[:])

@@ -9,7 +9,7 @@ ACT = mybir.ActivationFunctionType
 
 P = 128
 PER_COLUMN = 16
-PIECE = 512
+PIECE = 256
 
 
 def tile_quantuminspiredllm_kernel(tc, tok, pos, phase, offs, out):

@@ -24,13 +24,13 @@ def tile_quantuminspiredllm_kernel(tc, tok, pos, phase, offs, out):
     with (
         tc.tile_pool(name="held", bufs=1) as held,
         tc.tile_pool(name="work", bufs=blocks * sequences * spans) as work,
+        tc.psum_pool(name="psum", bufs=1) as psum,
     ):
         offsets = held.tile([P, entries // PER_COLUMN], U16, name="offsets")
         nc.sync.dma_start(offsets[:], offs)
 
-        phases = held.tile([P, blocks], F32, name="phases")
-        with nc.allow_non_contiguous_dma(reason="one float32 to a partition, 256 in all"):
-            nc.scalar.dma_start(phases[:], phase.rearrange("(b p) o -> p (b o)", p=P))
+        phase_row = held.tile([1, channels], F32, name="phase_row")
+        nc.scalar.dma_start(phase_row[:], phase.rearrange("c o -> o c"))
 
         tables = []
         positions = []
@@ -43,6 +43,12 @@ def tile_quantuminspiredllm_kernel(tc, tok, pos, phase, offs, out):
                 position = held.tile([P, PIECE], F32, name=f"position{b}_{h}")
                 nc.sync.dma_start(position[:], pos[rows, h * PIECE : (h + 1) * PIECE])
                 positions.append(position)
+
+        one = held.tile([1, 1], F32, name="one")
+        nc.vector.memset(one[:], 1.0)
+        phases = psum.tile([P, blocks], F32, name="phases")
+        for b in range(blocks):
+            nc.tensor.matmul(phases[:, b : b + 1], phase_row[:, b * P : (b + 1) * P], one[:])
 
         rot = held.tile([P, blocks], F32, name="rot")
         nc.scalar.activation(rot[:], phases[:], ACT.Tanh)

@@ -19,11 +19,9 @@ def tile_quantuminspiredllm_kernel(tc, tok, pos, phase, offs, out):
     entries = out.shape[1]
     blocks = channels // P
     sequences = entries // length
-    spans = length // PIECE
 
     with (
         tc.tile_pool(name="held", bufs=1) as held,
-        tc.tile_pool(name="work", bufs=blocks * sequences * spans) as work,
         tc.psum_pool(name="psum", bufs=1) as psum,
     ):
         offsets = held.tile([P, entries // PER_COLUMN], U16, name="offsets")
@@ -39,10 +37,10 @@ def tile_quantuminspiredllm_kernel(tc, tok, pos, phase, offs, out):
             table = held.tile([P, words], F32, name=f"table{b}")
             nc.sync.dma_start(table[:], tok[rows, :])
             tables.append(table)
-            for h in range(spans):
-                position = held.tile([P, PIECE], F32, name=f"position{b}_{h}")
-                nc.sync.dma_start(position[:], pos[rows, h * PIECE : (h + 1) * PIECE])
-                positions.append(position)
+            position = held.tile([P, length], F32, name=f"position{b}")
+            for h in range(0, length, PIECE):
+                nc.sync.dma_start(position[:, h : h + PIECE], pos[rows, h : h + PIECE])
+            positions.append(position)
 
         one = held.tile([1, 1], F32, name="one")
         nc.vector.memset(one[:], 1.0)
@@ -58,16 +56,17 @@ def tile_quantuminspiredllm_kernel(tc, tok, pos, phase, offs, out):
 
         for b in range(blocks):
             rows = slice(b * P, (b + 1) * P)
-            for h in range(spans):
+            result = held.tile([P, entries], F32, name=f"result{b}")
+            for start in range(0, length, PIECE):
                 for s in range(sequences):
-                    first = s * length + h * PIECE
-                    piece_offsets = offsets[:, first // PER_COLUMN : (first + PIECE) // PER_COLUMN]
-                    piece = work.tile([P, PIECE], F32, name="piece")
+                    first = s * length + start
+                    width = PIECE
+                    piece = slice(first, first + width)
                     nc.vector.tensor_tensor(
-                        piece[:],
-                        tables[b][:].indirect(piece_offsets),
-                        positions[b * spans + h][:],
+                        result[:, piece],
+                        tables[b][:].indirect(offsets[:, first // PER_COLUMN : (first + width) // PER_COLUMN]),
+                        positions[b][:, start : start + width],
                         ADD,
                     )
-                    nc.scalar.activation(piece[:], piece[:], ACT.Identity, scale=rot[:, b : b + 1])
-                    nc.sync.dma_start(out[rows, first : first + PIECE], piece[:])
+                    nc.scalar.activation(result[:, piece], result[:, piece], ACT.Identity, scale=rot[:, b : b + 1])
+                    nc.sync.dma_start(out[rows, piece], result[:, piece])

@@ -69,4 +69,7 @@ def tile_quantuminspiredllm_kernel(tc, tok, pos, phase, offs, out):
                         ADD,
                     )
                     nc.scalar.activation(result[:, piece], result[:, piece], ACT.Identity, scale=rot[:, b : b + 1])
-                    nc.sync.dma_start(out[rows, piece], result[:, piece])
+                    if b == blocks - 1:
+                        nc.sync.dma_start(out[rows, piece], result[:, piece])
+            if b < blocks - 1:
+                nc.sync.dma_start(out[rows, :], result[:])

@@ -35,11 +35,12 @@ def tile_quantuminspiredllm_kernel(tc, tok, pos, phase, offs, out):
         for b in range(blocks):
             rows = slice(b * P, (b + 1) * P)
             table = held.tile([P, words], F32, name=f"table{b}")
-            nc.sync.dma_start(table[:], tok[rows, :])
-            tables.append(table)
             position = held.tile([P, length], F32, name=f"position{b}")
-            for h in range(0, length, PIECE):
+            nc.sync.dma_start(position[:, :PIECE], pos[rows, :PIECE])
+            nc.sync.dma_start(table[:], tok[rows, :])
+            for h in range(PIECE, length, PIECE):
                 nc.sync.dma_start(position[:, h : h + PIECE], pos[rows, h : h + PIECE])
+            tables.append(table)
             positions.append(position)
 
         one = held.tile([1, 1], F32, name="one")

@@ -69,7 +69,10 @@ def tile_quantuminspiredllm_kernel(tc, tok, pos, phase, offs, out):
                         positions[b][:, start : start + width],
                         ADD,
                     )
-                    nc.scalar.activation(result[:, piece], result[:, piece], ACT.Identity, scale=rot[:, b : b + 1])
+                    if b == blocks - 1 and first + width == entries:
+                        nc.vector.tensor_scalar_mul(result[:, piece], result[:, piece], rot[:, b : b + 1])
+                    else:
+                        nc.scalar.activation(result[:, piece], result[:, piece], ACT.Identity, scale=rot[:, b : b + 1])
                     if b == blocks - 1:
                         nc.sync.dma_start(out[rows, piece], result[:, piece])
             if b < blocks - 1:

@@ -5,6 +5,7 @@ import concourse.mybir as mybir
 F32 = mybir.dt.float32
 U16 = mybir.dt.uint16
 ADD = mybir.AluOpType.add
+MULT = mybir.AluOpType.mult
 ACT = mybir.ActivationFunctionType
 
 P = 128
@@ -49,11 +50,19 @@ def tile_quantuminspiredllm_kernel(tc, tok, pos, phase, offs, out):
         for b in range(blocks):
             nc.tensor.matmul(phases[:, b : b + 1], phase_row[:, b * P : (b + 1) * P], one[:])
 
+        turn = held.tile([P, blocks], F32, name="turn")
+        half_sin = held.tile([P, blocks], F32, name="half_sin")
+        quarter_sin = held.tile([P, blocks], F32, name="quarter_sin")
+        nc.scalar.activation(turn[:], phases[:], ACT.Tanh)
+        nc.scalar.activation(half_sin[:], turn[:], ACT.Sin, scale=math.pi / 2)
+        nc.scalar.activation(quarter_sin[:], turn[:], ACT.Sin, scale=math.pi / 4)
+        half_cos = held.tile([P, blocks], F32, name="half_cos")
         rot = held.tile([P, blocks], F32, name="rot")
-        nc.scalar.activation(rot[:], phases[:], ACT.Tanh)
-        nc.scalar.activation(rot[:], rot[:], ACT.Abs, bias=0.25)
-        nc.scalar.activation(rot[:], rot[:], ACT.Sin, bias=math.pi / 2, scale=-math.pi)
-        nc.scalar.mul(rot[:], rot[:], math.sqrt(2.0))
+        nc.vector.tensor_tensor(half_cos[:], quarter_sin[:], quarter_sin[:], MULT)
+        nc.vector.tensor_scalar(half_cos[:], half_cos[:], -2.0, 1.0, MULT, ADD)
+        nc.vector.tensor_tensor(rot[:], half_sin[:], half_cos[:], ADD)
+        nc.vector.tensor_tensor(rot[:], rot[:], half_sin[:], MULT)
+        nc.vector.tensor_scalar(rot[:], rot[:], -2.0, 1.0, MULT, ADD)
 
         for b in range(blocks):
             rows = slice(b * P, (b + 1) * P)

@@ -11,6 +11,7 @@ ACT = mybir.ActivationFunctionType
 P = 128
 PER_COLUMN = 16
 PIECE = 256
+LEAD = PIECE // 2
 
 
 def tile_quantuminspiredllm_kernel(tc, tok, pos, phase, offs, out):
@@ -31,16 +32,18 @@ def tile_quantuminspiredllm_kernel(tc, tok, pos, phase, offs, out):
         phase_row = held.tile([1, channels], F32, name="phase_row")
         nc.scalar.dma_start(phase_row[:], phase.rearrange("c o -> o c"))
 
+        cuts = [0, LEAD] + list(range(2 * PIECE, length + 1, PIECE))
+        spans = list(zip(cuts[:-1], cuts[1:]))
         tables = []
         positions = []
         for b in range(blocks):
             rows = slice(b * P, (b + 1) * P)
             table = held.tile([P, words], F32, name=f"table{b}")
             position = held.tile([P, length], F32, name=f"position{b}")
-            nc.sync.dma_start(position[:, :PIECE], pos[rows, :PIECE])
+            nc.sync.dma_start(position[:, :LEAD], pos[rows, :LEAD])
             nc.sync.dma_start(table[:], tok[rows, :])
-            for h in range(PIECE, length, PIECE):
-                nc.sync.dma_start(position[:, h : h + PIECE], pos[rows, h : h + PIECE])
+            for start, end in spans[1:]:
+                nc.sync.dma_start(position[:, start:end], pos[rows, start:end])
             tables.append(table)
             positions.append(position)
 
@@ -67,22 +70,26 @@ def tile_quantuminspiredllm_kernel(tc, tok, pos, phase, offs, out):
         for b in range(blocks):
             rows = slice(b * P, (b + 1) * P)
             result = held.tile([P, entries], F32, name=f"result{b}")
-            for start in range(0, length, PIECE):
+            for start, end in spans:
                 for s in range(sequences):
                     first = s * length + start
-                    width = PIECE
-                    piece = slice(first, first + width)
-                    nc.vector.tensor_tensor(
-                        result[:, piece],
-                        tables[b][:].indirect(offsets[:, first // PER_COLUMN : (first + width) // PER_COLUMN]),
-                        positions[b][:, start : start + width],
-                        ADD,
-                    )
-                    if b == blocks - 1 and first + width == entries:
-                        nc.vector.tensor_scalar_mul(result[:, piece], result[:, piece], rot[:, b : b + 1])
-                    else:
-                        nc.scalar.activation(result[:, piece], result[:, piece], ACT.Identity, scale=rot[:, b : b + 1])
-                    if b == blocks - 1:
-                        nc.sync.dma_start(out[rows, piece], result[:, piece])
+                    very_last = b == blocks - 1 and first + end - start == entries
+                    width = (end - start) // 2 if very_last else end - start
+                    for offset in range(0, end - start, width):
+                        piece = slice(first + offset, first + offset + width)
+                        nc.vector.tensor_tensor(
+                            result[:, piece],
+                            tables[b][:].indirect(offsets[:, piece.start // PER_COLUMN : piece.stop // PER_COLUMN]),
+                            positions[b][:, start + offset : start + offset + width],
+                            ADD,
+                        )
+                        if b == blocks - 1 and piece.stop == entries:
+                            nc.vector.tensor_scalar_mul(result[:, piece], result[:, piece], rot[:, b : b + 1])
+                        else:
+                            nc.scalar.activation(
+                                result[:, piece], result[:, piece], ACT.Identity, scale=rot[:, b : b + 1]
+                            )
+                        if b == blocks - 1:
+                            nc.sync.dma_start(out[rows, piece], result[:, piece])
             if b < blocks - 1:
                 nc.sync.dma_start(out[rows, :], result[:])

@@ -10,8 +10,7 @@ ACT = mybir.ActivationFunctionType
 
 P = 128
 PER_COLUMN = 16
-PIECE = 256
-LEAD = PIECE // 2
+LEAD = 128
 
 
 def tile_quantuminspiredllm_kernel(tc, tok, pos, phase, offs, out):
@@ -32,20 +31,17 @@ def tile_quantuminspiredllm_kernel(tc, tok, pos, phase, offs, out):
         phase_row = held.tile([1, channels], F32, name="phase_row")
         nc.scalar.dma_start(phase_row[:], phase.rearrange("c o -> o c"))
 
-        cuts = [0, LEAD] + list(range(2 * PIECE, length + 1, PIECE))
-        spans = list(zip(cuts[:-1], cuts[1:]))
+        half = length // 2
+        pos_by_block = pos.rearrange("(b p) t -> p b t", p=P)
+        positions = held.tile([P, blocks, length], F32, name="positions")
+        nc.sync.dma_start(positions[:, :, :LEAD], pos_by_block[:, :, :LEAD])
         tables = []
-        positions = []
         for b in range(blocks):
-            rows = slice(b * P, (b + 1) * P)
             table = held.tile([P, words], F32, name=f"table{b}")
-            position = held.tile([P, length], F32, name=f"position{b}")
-            nc.sync.dma_start(position[:, :LEAD], pos[rows, :LEAD])
-            nc.sync.dma_start(table[:], tok[rows, :])
-            for start, end in spans[1:]:
-                nc.sync.dma_start(position[:, start:end], pos[rows, start:end])
+            nc.sync.dma_start(table[:], tok[b * P : (b + 1) * P, :])
+            for start, end in [(LEAD, length)] if b < blocks - 1 else [(LEAD, half), (half, length)]:
+                nc.sync.dma_start(positions[:, b, start:end], pos_by_block[:, b, start:end])
             tables.append(table)
-            positions.append(position)
 
         one = held.tile([1, 1], F32, name="one")
         nc.vector.memset(one[:], 1.0)
@@ -68,28 +64,28 @@ def tile_quantuminspiredllm_kernel(tc, tok, pos, phase, offs, out):
         nc.vector.tensor_scalar(rot[:], rot[:], -2.0, 1.0, MULT, ADD)
 
         for b in range(blocks):
+            last_block = b == blocks - 1
             rows = slice(b * P, (b + 1) * P)
             result = held.tile([P, entries], F32, name=f"result{b}")
-            for start, end in spans:
-                for s in range(sequences):
-                    first = s * length + start
-                    very_last = b == blocks - 1 and first + end - start == entries
-                    width = (end - start) // 2 if very_last else end - start
-                    for offset in range(0, end - start, width):
-                        piece = slice(first + offset, first + offset + width)
-                        nc.vector.tensor_tensor(
-                            result[:, piece],
-                            tables[b][:].indirect(offsets[:, piece.start // PER_COLUMN : piece.stop // PER_COLUMN]),
-                            positions[b][:, start + offset : start + offset + width],
-                            ADD,
-                        )
-                        if b == blocks - 1 and piece.stop == entries:
-                            nc.vector.tensor_scalar_mul(result[:, piece], result[:, piece], rot[:, b : b + 1])
-                        else:
-                            nc.scalar.activation(
-                                result[:, piece], result[:, piece], ACT.Identity, scale=rot[:, b : b + 1]
-                            )
-                        if b == blocks - 1:
-                            nc.sync.dma_start(out[rows, piece], result[:, piece])
-            if b < blocks - 1:
+            cuts = [0, LEAD, half, length - 2 * LEAD, length] if last_block else [0, LEAD, half, length]
+            pieces = [(s * length, start, end) for start, end in zip(cuts[:-1], cuts[1:]) for s in range(sequences)]
+            if last_block:
+                base, start, end = pieces.pop()
+                pieces += [(base, start, end - LEAD), (base, end - LEAD, end)]
+            for base, start, end in pieces:
+                piece = slice(base + start, base + end)
+                nc.vector.tensor_tensor(
+                    result[:, piece],
+                    tables[b][:].indirect(offsets[:, piece.start // PER_COLUMN : piece.stop // PER_COLUMN]),
+                    positions[:, b, start:end],
+                    ADD,
+                )
+                if last_block and piece.stop == entries:
+                    nc.vector.tensor_scalar_mul(result[:, piece], result[:, piece], rot[:, b : b + 1])
+                else:
+                    nc.scalar.activation(result[:, piece], result[:, piece], ACT.Identity, scale=rot[:, b : b + 1])
+                if last_block and start > 0:
+                    begin = base if start == LEAD else piece.start
+                    nc.sync.dma_start(out[rows, begin : piece.stop], result[:, begin : piece.stop])
+            if not last_block:
                 nc.sync.dma_start(out[rows, :], result[:])

@@ -29,7 +29,9 @@ def tile_quantuminspiredllm_kernel(tc, tok, pos, phase, offs, out):
         nc.sync.dma_start(offsets[:], offs)
 
         phase_row = held.tile([1, channels], F32, name="phase_row")
-        nc.scalar.dma_start(phase_row[:], phase.rearrange("c o -> o c"))
+        for b in range(blocks):
+            columns = slice(b * P, (b + 1) * P)
+            nc.scalar.dma_start(phase_row[:, columns], phase[columns, :].rearrange("c o -> o c"))
 
         half = length // 2
         pos_by_block = pos.rearrange("(b p) t -> p b t", p=P)
@@ -84,8 +86,12 @@ def tile_quantuminspiredllm_kernel(tc, tok, pos, phase, offs, out):
                     nc.vector.tensor_scalar_mul(result[:, piece], result[:, piece], rot[:, b : b + 1])
                 else:
                     nc.scalar.activation(result[:, piece], result[:, piece], ACT.Identity, scale=rot[:, b : b + 1])
-                if last_block and start > 0:
-                    begin = base if start == LEAD else piece.start
-                    nc.sync.dma_start(out[rows, begin : piece.stop], result[:, begin : piece.stop])
+                if last_block and start >= half:
+                    nc.sync.dma_start(out[rows, piece], result[:, piece])
+                elif last_block and piece.stop == entries - half:
+                    nc.sync.dma_start(
+                        out[rows, :].rearrange("c (s t) -> c s t", s=sequences)[:, :, :half],
+                        result[:].rearrange("c (s t) -> c s t", s=sequences)[:, :, :half],
+                    )
             if not last_block:
                 nc.sync.dma_start(out[rows, :], result[:])

@@ -25,9 +25,6 @@ def tile_quantuminspiredllm_kernel(tc, tok, pos, phase, offs, out):
         tc.tile_pool(name="held", bufs=1) as held,
         tc.psum_pool(name="psum", bufs=1) as psum,
     ):
-        offsets = held.tile([P, entries // PER_COLUMN], U16, name="offsets")
-        nc.sync.dma_start(offsets[:], offs)
-
         phase_row = held.tile([1, channels], F32, name="phase_row")
         for b in range(blocks):
             columns = slice(b * P, (b + 1) * P)
@@ -37,6 +34,8 @@ def tile_quantuminspiredllm_kernel(tc, tok, pos, phase, offs, out):
         pos_by_block = pos.rearrange("(b p) t -> p b t", p=P)
         positions = held.tile([P, blocks, length], F32, name="positions")
         nc.sync.dma_start(positions[:, :, :LEAD], pos_by_block[:, :, :LEAD])
+        offsets = held.tile([P, entries // PER_COLUMN], U16, name="offsets")
+        nc.sync.dma_start(offsets[:], offs)
         tables = []
         for b in range(blocks):
             table = held.tile([P, words], F32, name=f"table{b}")

import math

import concourse.mybir as mybir

F32 = mybir.dt.float32
U16 = mybir.dt.uint16
ADD = mybir.AluOpType.add
MULT = mybir.AluOpType.mult
ACT = mybir.ActivationFunctionType

P = 128
PER_COLUMN = 16
LEAD = 128


def tile_quantuminspiredllm_kernel(tc, tok, pos, phase, offs, out):
    nc = tc.nc
    channels, words = tok.shape
    length = pos.shape[1]
    entries = out.shape[1]
    blocks = channels // P
    sequences = entries // length

    with (
        tc.tile_pool(name="held", bufs=1) as held,
        tc.psum_pool(name="psum", bufs=1) as psum,
    ):
        phase_row = held.tile([1, channels], F32, name="phase_row")
        for b in range(blocks):
            columns = slice(b * P, (b + 1) * P)
            nc.scalar.dma_start(phase_row[:, columns], phase[columns, :].rearrange("c o -> o c"))

        half = length // 2
        pos_by_block = pos.rearrange("(b p) t -> p b t", p=P)
        positions = held.tile([P, blocks, length], F32, name="positions")
        nc.sync.dma_start(positions[:, :, :LEAD], pos_by_block[:, :, :LEAD])
        offsets = held.tile([P, entries // PER_COLUMN], U16, name="offsets")
        nc.sync.dma_start(offsets[:], offs)
        tables = []
        for b in range(blocks):
            table = held.tile([P, words], F32, name=f"table{b}")
            nc.sync.dma_start(table[:], tok[b * P : (b + 1) * P, :])
            for start, end in [(LEAD, length)] if b < blocks - 1 else [(LEAD, half), (half, length)]:
                nc.sync.dma_start(positions[:, b, start:end], pos_by_block[:, b, start:end])
            tables.append(table)

        one = held.tile([1, 1], F32, name="one")
        nc.vector.memset(one[:], 1.0)
        phases = psum.tile([P, blocks], F32, name="phases")
        for b in range(blocks):
            nc.tensor.matmul(phases[:, b : b + 1], phase_row[:, b * P : (b + 1) * P], one[:])

        turn = held.tile([P, blocks], F32, name="turn")
        half_sin = held.tile([P, blocks], F32, name="half_sin")
        quarter_sin = held.tile([P, blocks], F32, name="quarter_sin")
        nc.scalar.activation(turn[:], phases[:], ACT.Tanh)
        nc.scalar.activation(half_sin[:], turn[:], ACT.Sin, scale=math.pi / 2)
        nc.scalar.activation(quarter_sin[:], turn[:], ACT.Sin, scale=math.pi / 4)
        half_cos = held.tile([P, blocks], F32, name="half_cos")
        rot = held.tile([P, blocks], F32, name="rot")
        nc.vector.tensor_tensor(half_cos[:], quarter_sin[:], quarter_sin[:], MULT)
        nc.vector.tensor_scalar(half_cos[:], half_cos[:], -2.0, 1.0, MULT, ADD)
        nc.vector.tensor_tensor(rot[:], half_sin[:], half_cos[:], ADD)
        nc.vector.tensor_tensor(rot[:], rot[:], half_sin[:], MULT)
        nc.vector.tensor_scalar(rot[:], rot[:], -2.0, 1.0, MULT, ADD)

        for b in range(blocks):
            last_block = b == blocks - 1
            rows = slice(b * P, (b + 1) * P)
            result = held.tile([P, entries], F32, name=f"result{b}")
            cuts = [0, LEAD, half, length - 2 * LEAD, length] if last_block else [0, LEAD, half, length]
            pieces = [(s * length, start, end) for start, end in zip(cuts[:-1], cuts[1:]) for s in range(sequences)]
            if last_block:
                base, start, end = pieces.pop()
                pieces += [(base, start, end - LEAD), (base, end - LEAD, end)]
            for base, start, end in pieces:
                piece = slice(base + start, base + end)
                nc.vector.tensor_tensor(
                    result[:, piece],
                    tables[b][:].indirect(offsets[:, piece.start // PER_COLUMN : piece.stop // PER_COLUMN]),
                    positions[:, b, start:end],
                    ADD,
                )
                if last_block and piece.stop == entries:
                    nc.vector.tensor_scalar_mul(result[:, piece], result[:, piece], rot[:, b : b + 1])
                else:
                    nc.scalar.activation(result[:, piece], result[:, piece], ACT.Identity, scale=rot[:, b : b + 1])
                if last_block and start >= half:
                    nc.sync.dma_start(out[rows, piece], result[:, piece])
                elif last_block and piece.stop == entries - half:
                    nc.sync.dma_start(
                        out[rows, :].rearrange("c (s t) -> c s t", s=sequences)[:, :, :half],
                        result[:].rearrange("c (s t) -> c s t", s=sequences)[:, :, :half],
                    )
            if not last_block:
                nc.sync.dma_start(out[rows, :], result[:])
